import numpy as np
import ml_dtypes


def mxq(x, axis, fmt="e4m3"):
    dtype, down = {"e4m3": (ml_dtypes.float8_e4m3fn, 7), "e5m2": (ml_dtypes.float8_e5m2, 14)}[fmt]
    v = np.moveaxis(np.asarray(x, np.float32).astype(ml_dtypes.bfloat16).astype(np.float64), axis, -1)
    blocks = v.reshape(v.shape[:-1] + (-1, 32))
    amax = np.abs(blocks).max(-1, keepdims=True)
    byte = np.maximum(np.where(amax > 0, np.frexp(amax)[1] - 1 + 127, 0) - down, 1)
    scale = np.exp2(byte - 127.0)
    codes = (blocks / scale).astype(np.float32).astype(dtype).astype(np.float64)
    return np.moveaxis((codes * scale).reshape(v.shape), -1, axis)


WIDE = False


def mx_kscale(k):
    if not WIDE:
        return np.ones(k)
    levels = np.array([20, -20, 10, -10, 0])
    a = np.random.permutation(np.resize(levels, k // 512 * 4)).reshape(k // 512, 4)
    idx = np.arange(k)
    return np.exp2(a[idx // 512, idx % 128 // 32])


BF16 = ml_dtypes.bfloat16


def bf(x):
    return np.asarray(x, np.float32).astype(BF16)


def f64(x):
    return np.asarray(x).astype(np.float64)


B, K, D, H1, H2, C = 512, 2, 2048, 1024, 512, 64
N = B * K


def preact(nf1, nf2, w1_0, w2_0):
    n, d = nf1.shape
    agg = nf2.reshape(n, -1, d).mean(axis=1)
    return nf1 @ w2_0 + agg @ w1_0


def setup_inputs():
    s = mx_kscale(N)[:, None]
    nf1_0 = bf(np.random.standard_normal((N, D)))
    nf2 = bf(np.random.standard_normal((N * K, D)))
    w1_0 = bf(np.random.standard_normal((D, H1)) / np.sqrt(D))
    w2_0 = bf(np.random.standard_normal((D, H1)) / np.sqrt(D))
    g = bf(np.random.standard_normal((N, H1)) * np.exp2(np.random.randint(-12, 1, (N, 1))) / s)
    z = preact(f64(nf1_0), f64(nf2), f64(w1_0), f64(w2_0))
    return {"nf1": bf(f64(nf1_0) * s), "nf2": nf2, "w1_0": w1_0, "w2_0": w2_0,
            "z": np.asarray(z, np.float32), "grad_out": g}


def reference(nf1, nf2, w1_0, w2_0, z, grad_out):
    dz = np.where(f64(z) > 0.0, f64(grad_out), 0.0)
    return mxq(f64(nf1), 0, "e4m3").T @ mxq(dz, 0, "e5m2")

@@ -1,0 +1,138 @@
+from contextlib import ExitStack
+
+import concourse.mybir as mybir
+
+F32 = mybir.dt.float32
+BF16 = mybir.dt.bfloat16
+U32 = mybir.dt.uint32
+U8 = mybir.dt.uint8
+E4M3_X4 = mybir.dt.float8_e4m3fn_x4
+E5M2_X4 = mybir.dt.float8_e5m2_x4
+ALU = mybir.AluOpType
+
+P = 128
+PACK = 4
+K_PASS = P * PACK
+
+NODES = 1024
+D = 2048
+H = 1024
+PASSES = NODES // K_PASS
+
+H_PIECE = 512
+H_PIECES = H // H_PIECE
+D_BLOCK = P
+D_CHUNK = 512
+BLOCKS_PER_CHUNK = D_CHUNK // D_BLOCK
+D_CHUNKS = D // D_CHUNK
+D_BLOCKS = D // D_BLOCK
+
+FLOPS = 2 * NODES * D * H
+BYTES = NODES * D * 2 + NODES * H * 4 + NODES * H * 2 + D * H * 4
+
+
+def tile_graphsage_pa_v_kernel(tc, nf1, nf2, w1_0, w2_0, z, grad_out, out):
+    nc = tc.nc
+
+    z_rows = z.rearrange("(c p j) h -> c p j h", p=P, j=PACK)
+    g_rows = grad_out.rearrange("(c p j) h -> c p j h", p=P, j=PACK)
+    nf1_rows = nf1.rearrange("(c p j) d -> c p j d", p=P, j=PACK)
+
+    with ExitStack() as ctx:
+        loads = ctx.enter_context(tc.tile_pool(name="loads", bufs=PASSES * H_PIECES))
+        grouped = ctx.enter_context(tc.tile_pool(name="grouped", bufs=3))
+        dz_mx = ctx.enter_context(tc.tile_pool(name="dz_mx", bufs=PASSES * H_PIECES))
+        nf1_mx = ctx.enter_context(tc.tile_pool(name="nf1_mx", bufs=4))
+        results = ctx.enter_context(tc.tile_pool(name="results", bufs=4))
+        psum = ctx.enter_context(tc.psum_pool(name="psum", bufs=8))
+
+        dz_pieces = [(c, n) for c in range(PASSES) for n in range(H_PIECES)]
+        z_raw = {}
+        g_raw = {}
+        for c, n in dz_pieces:
+            h_cols = slice(n * H_PIECE, (n + 1) * H_PIECE)
+            g_tile = loads.tile([P, PACK, H_PIECE], BF16, tag="g_raw")
+            nc.sync.dma_start(out=g_tile[:], in_=g_rows[c, :, :, h_cols])
+            z_tile = loads.tile([P, PACK, H_PIECE], F32, tag="z_raw")
+            nc.sync.dma_start(out=z_tile[:], in_=z_rows[c, :, :, h_cols])
+            g_raw[(c, n)] = g_tile
+            z_raw[(c, n)] = z_tile
+        nf1_raw = []
+        for q in range(D_CHUNKS):
+            d_cols = slice(q * D_CHUNK, (q + 1) * D_CHUNK)
+            nf1_tile = loads.tile([P, PASSES, PACK, D_CHUNK], BF16, tag="nf1_raw")
+            for c in range(PASSES):
+                nc.sync.dma_start(out=nf1_tile[:, c, :, :], in_=nf1_rows[c, :, :, d_cols])
+            nf1_raw.append(nf1_tile)
+
+        def mask_piece(c, n):
+            dz_grouped = grouped.tile([P, H_PIECE, PACK], BF16, align_bytes=64)
+            nc.vector.scalar_tensor_tensor(
+                out=dz_grouped[:],
+                in0=z_raw[(c, n)][:].rearrange("p j h -> p h j"),
+                scalar=0.0,
+                in1=g_raw[(c, n)][:].rearrange("p j h -> p h j"),
+                op0=ALU.is_gt,
+                op1=ALU.mult,
+            )
+            return dz_grouped
+
+        dz_codes = {}
+        dz_scales = {}
+
+        def quantise_piece(c, n, dz_grouped):
+            codes = dz_mx.tile([P, H_PIECE], U32, tag="dz_codes", align_bytes=64)
+            scales = dz_mx.tile([P, H_PIECE], U8, tag="dz_scales", align_bytes=64)
+            nc.vector.quantize_mx(
+                out=codes[:].bitcast(E5M2_X4),
+                scales=scales[:],
+                in_=dz_grouped[:].rearrange("p h j -> p (h j)"),
+            )
+            dz_codes[(c, n)] = codes
+            dz_scales[(c, n)] = scales
+
+        def regroup_block(b):
+            q, i = divmod(b, BLOCKS_PER_CHUNK)
+            nf1_grouped = grouped.tile([P, PASSES, D_BLOCK, PACK], BF16, align_bytes=64)
+            nc.vector.tensor_copy(
+                out=nf1_grouped[:],
+                in_=nf1_raw[q][:, :, :, i * D_BLOCK : (i + 1) * D_BLOCK].rearrange("p c j d -> p c d j"),
+            )
+            return nf1_grouped
+
+        filled = None
+        for c, n in dz_pieces:
+            now_filled = (c, n, mask_piece(c, n))
+            if filled is not None:
+                quantise_piece(*filled)
+            filled = now_filled
+        next_grouped = regroup_block(0)
+        quantise_piece(*filled)
+
+        for b in range(D_BLOCKS):
+            nf1_grouped = next_grouped
+            if b + 1 < D_BLOCKS:
+                next_grouped = regroup_block(b + 1)
+            nf1_codes = nf1_mx.tile([P, PASSES, D_BLOCK], U32, align_bytes=64)
+            nf1_scales = nf1_mx.tile([P, PASSES, D_BLOCK], U8, align_bytes=64)
+            nc.vector.quantize_mx(
+                out=nf1_codes[:].rearrange("p c d -> p (c d)").bitcast(E4M3_X4),
+                scales=nf1_scales[:].rearrange("p c d -> p (c d)"),
+                in_=nf1_grouped[:].rearrange("p c d j -> p (c d j)"),
+            )
+
+            result = results.tile([P, H], F32)
+            for n in range(H_PIECES):
+                acc = psum.tile([P, H_PIECE], F32)
+                for c in range(PASSES):
+                    nc.tensor.matmul_mx(
+                        out=acc[:],
+                        lhsT=nf1_codes[:, c, :].bitcast(E4M3_X4),
+                        lhsT_scale=nf1_scales[:, c, :],
+                        rhs=dz_codes[(c, n)][:].bitcast(E5M2_X4),
+                        rhs_scale=dz_scales[(c, n)][:],
+                        start=(c == 0),
+                        stop=(c == PASSES - 1),
+                    )
+                nc.scalar.copy(out=result[:, n * H_PIECE : (n + 1) * H_PIECE], in_=acc[:])
+            nc.sync.dma_start(out=out[b * D_BLOCK : (b + 1) * D_BLOCK, :], in_=result[:])

@@ -22,10 +22,8 @@ PASSES = NODES // K_PASS
 H_PIECE = 512
 H_PIECES = H // H_PIECE
 D_BLOCK = P
-D_CHUNK = 512
-BLOCKS_PER_CHUNK = D_CHUNK // D_BLOCK
-D_CHUNKS = D // D_CHUNK
 D_BLOCKS = D // D_BLOCK
+D_FIRST_CHUNK = 512
 
 FLOPS = 2 * NODES * D * H
 BYTES = NODES * D * 2 + NODES * H * 4 + NODES * H * 2 + D * H * 4
@@ -39,7 +37,7 @@ def tile_graphsage_pa_v_kernel(tc, nf1, nf2, w1_0, w2_0, z, grad_out, out):
     nf1_rows = nf1.rearrange("(c p j) d -> c p j d", p=P, j=PACK)
 
     with ExitStack() as ctx:
-        loads = ctx.enter_context(tc.tile_pool(name="loads", bufs=PASSES * H_PIECES))
+        loads = ctx.enter_context(tc.tile_pool(name="loads", bufs=1))
         grouped = ctx.enter_context(tc.tile_pool(name="grouped", bufs=3))
         dz_mx = ctx.enter_context(tc.tile_pool(name="dz_mx", bufs=PASSES * H_PIECES))
         nf1_mx = ctx.enter_context(tc.tile_pool(name="nf1_mx", bufs=4))
@@ -49,21 +47,27 @@ def tile_graphsage_pa_v_kernel(tc, nf1, nf2, w1_0, w2_0, z, grad_out, out):
         dz_pieces = [(c, n) for c in range(PASSES) for n in range(H_PIECES)]
         z_raw = {}
         g_raw = {}
-        for c, n in dz_pieces:
-            h_cols = slice(n * H_PIECE, (n + 1) * H_PIECE)
-            g_tile = loads.tile([P, PACK, H_PIECE], BF16, tag="g_raw")
-            nc.sync.dma_start(out=g_tile[:], in_=g_rows[c, :, :, h_cols])
-            z_tile = loads.tile([P, PACK, H_PIECE], F32, tag="z_raw")
-            nc.sync.dma_start(out=z_tile[:], in_=z_rows[c, :, :, h_cols])
-            g_raw[(c, n)] = g_tile
-            z_raw[(c, n)] = z_tile
-        nf1_raw = []
-        for q in range(D_CHUNKS):
-            d_cols = slice(q * D_CHUNK, (q + 1) * D_CHUNK)
-            nf1_tile = loads.tile([P, PASSES, PACK, D_CHUNK], BF16, tag="nf1_raw")
+        for c in range(PASSES):
+            g_raw[c] = loads.tile([P, PACK, H], BF16, name="g_raw_%d" % c)
+            nc.sync.dma_start(out=g_raw[c][:], in_=g_rows[c])
+            for n in range(H_PIECES):
+                z_raw[(c, n)] = loads.tile([P, PACK, H_PIECE], F32, name="z_raw_%d_%d" % (c, n))
+                nc.sync.dma_start(
+                    out=z_raw[(c, n)][:], in_=z_rows[c, :, :, n * H_PIECE : (n + 1) * H_PIECE]
+                )
+        nf1_source = {}
+        first_col = 0
+        width = D_FIRST_CHUNK
+        while first_col < D:
+            nf1_tile = loads.tile([P, PASSES, PACK, width], BF16, name="nf1_raw_%d" % first_col)
             for c in range(PASSES):
-                nc.sync.dma_start(out=nf1_tile[:, c, :, :], in_=nf1_rows[c, :, :, d_cols])
-            nf1_raw.append(nf1_tile)
+                nc.sync.dma_start(
+                    out=nf1_tile[:, c, :, :], in_=nf1_rows[c, :, :, first_col : first_col + width]
+                )
+            for col in range(0, width, D_BLOCK):
+                nf1_source[(first_col + col) // D_BLOCK] = (nf1_tile, col)
+            first_col += width
+            width = first_col
 
         def mask_piece(c, n):
             dz_grouped = grouped.tile([P, H_PIECE, PACK], BF16, align_bytes=64)
@@ -71,7 +75,7 @@ def tile_graphsage_pa_v_kernel(tc, nf1, nf2, w1_0, w2_0, z, grad_out, out):
                 out=dz_grouped[:],
                 in0=z_raw[(c, n)][:].rearrange("p j h -> p h j"),
                 scalar=0.0,
-                in1=g_raw[(c, n)][:].rearrange("p j h -> p h j"),
+                in1=g_raw[c][:, :, n * H_PIECE : (n + 1) * H_PIECE].rearrange("p j h -> p h j"),
                 op0=ALU.is_gt,
                 op1=ALU.mult,
             )
@@ -92,11 +96,11 @@ def tile_graphsage_pa_v_kernel(tc, nf1, nf2, w1_0, w2_0, z, grad_out, out):
             dz_scales[(c, n)] = scales
 
         def regroup_block(b):
-            q, i = divmod(b, BLOCKS_PER_CHUNK)
+            nf1_tile, col = nf1_source[b]
             nf1_grouped = grouped.tile([P, PASSES, D_BLOCK, PACK], BF16, align_bytes=64)
             nc.vector.tensor_copy(
                 out=nf1_grouped[:],
-                in_=nf1_raw[q][:, :, :, i * D_BLOCK : (i + 1) * D_BLOCK].rearrange("p c j d -> p c d j"),
+                in_=nf1_tile[:, :, :, col : col + D_BLOCK].rearrange("p c j d -> p c d j"),
             )
             return nf1_grouped
 

@@ -21,6 +21,8 @@ PASSES = NODES // K_PASS
 
 H_PIECE = 512
 H_PIECES = H // H_PIECE
+MASK_COLS = 256
+RUN = 4
 D_BLOCK = P
 D_BLOCKS = D // D_BLOCK
 D_FIRST_CHUNK = 512
@@ -70,15 +72,22 @@ def tile_graphsage_pa_v_kernel(tc, nf1, nf2, w1_0, w2_0, z, grad_out, out):
             width = first_col
 
         def mask_piece(c, n):
+            dz_rows = grouped.tile([P, PACK, H_PIECE], BF16)
             dz_grouped = grouped.tile([P, H_PIECE, PACK], BF16, align_bytes=64)
-            nc.vector.scalar_tensor_tensor(
-                out=dz_grouped[:],
-                in0=z_raw[(c, n)][:].rearrange("p j h -> p h j"),
-                scalar=0.0,
-                in1=g_raw[c][:, :, n * H_PIECE : (n + 1) * H_PIECE].rearrange("p j h -> p h j"),
-                op0=ALU.is_gt,
-                op1=ALU.mult,
-            )
+            for first in range(0, H_PIECE, MASK_COLS):
+                cols = slice(first, first + MASK_COLS)
+                nc.vector.scalar_tensor_tensor(
+                    out=dz_rows[:, :, cols],
+                    in0=z_raw[(c, n)][:, :, cols],
+                    scalar=0.0,
+                    in1=g_raw[c][:, :, n * H_PIECE + first : n * H_PIECE + first + MASK_COLS],
+                    op0=ALU.is_gt,
+                    op1=ALU.mult,
+                )
+                nc.scalar.copy(
+                    out=dz_grouped[:, cols, :].rearrange("p (x i) j -> p x j i", i=RUN),
+                    in_=dz_rows[:, :, cols].rearrange("p j (x i) -> p x j i", i=RUN),
+                )
             return dz_grouped
 
         dz_codes = {}

@@ -25,7 +25,7 @@ MASK_COLS = 256
 RUN = 4
 D_BLOCK = P
 D_BLOCKS = D // D_BLOCK
-D_FIRST_CHUNK = 512
+D_FIRST_CHUNK = 256
 
 FLOPS = 2 * NODES * D * H
 BYTES = NODES * D * 2 + NODES * H * 4 + NODES * H * 2 + D * H * 4
@@ -46,17 +46,23 @@ def tile_graphsage_pa_v_kernel(tc, nf1, nf2, w1_0, w2_0, z, grad_out, out):
         results = ctx.enter_context(tc.tile_pool(name="results", bufs=4))
         psum = ctx.enter_context(tc.psum_pool(name="psum", bufs=8))
 
-        dz_pieces = [(c, n) for c in range(PASSES) for n in range(H_PIECES)]
-        z_raw = {}
-        g_raw = {}
-        for c in range(PASSES):
-            g_raw[c] = loads.tile([P, PACK, H], BF16, name="g_raw_%d" % c)
-            nc.sync.dma_start(out=g_raw[c][:], in_=g_rows[c])
-            for n in range(H_PIECES):
-                z_raw[(c, n)] = loads.tile([P, PACK, H_PIECE], F32, name="z_raw_%d_%d" % (c, n))
-                nc.sync.dma_start(
-                    out=z_raw[(c, n)][:], in_=z_rows[c, :, :, n * H_PIECE : (n + 1) * H_PIECE]
-                )
+        z_source = {}
+        g_source = {}
+
+        def load_columns(source, rows, dtype, c, first, width, label):
+            raw = loads.tile([P, PACK, width], dtype, name="%s_raw_%d_%d" % (label, c, first))
+            nc.sync.dma_start(out=raw[:], in_=rows[c, :, :, first : first + width])
+            for col in range(0, width, MASK_COLS):
+                source[(c, first + col)] = (raw, col)
+
+        load_columns(g_source, g_rows, BF16, 0, 0, H, "g")
+        load_columns(z_source, z_rows, F32, 0, 0, H_PIECE, "z")
+        load_columns(z_source, z_rows, F32, 0, H_PIECE, H_PIECE, "z")
+        load_columns(g_source, g_rows, BF16, 1, 0, H_PIECE, "g")
+        load_columns(z_source, z_rows, F32, 1, 0, H_PIECE, "z")
+        load_columns(g_source, g_rows, BF16, 1, H_PIECE, H_PIECE, "g")
+        load_columns(z_source, z_rows, F32, 1, H_PIECE, MASK_COLS, "z")
+        load_columns(z_source, z_rows, F32, 1, H_PIECE + MASK_COLS, MASK_COLS, "z")
         nf1_source = {}
         first_col = 0
         width = D_FIRST_CHUNK
@@ -76,11 +82,13 @@ def tile_graphsage_pa_v_kernel(tc, nf1, nf2, w1_0, w2_0, z, grad_out, out):
             dz_grouped = grouped.tile([P, H_PIECE, PACK], BF16, align_bytes=64)
             for first in range(0, H_PIECE, MASK_COLS):
                 cols = slice(first, first + MASK_COLS)
+                z_tile, z_col = z_source[(c, n * H_PIECE + first)]
+                g_tile, g_col = g_source[(c, n * H_PIECE + first)]
                 nc.vector.scalar_tensor_tensor(
                     out=dz_rows[:, :, cols],
-                    in0=z_raw[(c, n)][:, :, cols],
+                    in0=z_tile[:, :, z_col : z_col + MASK_COLS],
                     scalar=0.0,
-                    in1=g_raw[c][:, :, n * H_PIECE + first : n * H_PIECE + first + MASK_COLS],
+                    in1=g_tile[:, :, g_col : g_col + MASK_COLS],
                     op0=ALU.is_gt,
                     op1=ALU.mult,
                 )
@@ -113,19 +121,10 @@ def tile_graphsage_pa_v_kernel(tc, nf1, nf2, w1_0, w2_0, z, grad_out, out):
             )
             return nf1_grouped
 
-        filled = None
-        for c, n in dz_pieces:
-            now_filled = (c, n, mask_piece(c, n))
-            if filled is not None:
-                quantise_piece(*filled)
-            filled = now_filled
-        next_grouped = regroup_block(0)
-        quantise_piece(*filled)
+        block_codes = {}
+        block_scales = {}
 
-        for b in range(D_BLOCKS):
-            nf1_grouped = next_grouped
-            if b + 1 < D_BLOCKS:
-                next_grouped = regroup_block(b + 1)
+        def quantise_block(b, nf1_grouped):
             nf1_codes = nf1_mx.tile([P, PASSES, D_BLOCK], U32, align_bytes=64)
             nf1_scales = nf1_mx.tile([P, PASSES, D_BLOCK], U8, align_bytes=64)
             nc.vector.quantize_mx(
@@ -133,19 +132,44 @@ def tile_graphsage_pa_v_kernel(tc, nf1, nf2, w1_0, w2_0, z, grad_out, out):
                 scales=nf1_scales[:].rearrange("p c d -> p (c d)"),
                 in_=nf1_grouped[:].rearrange("p c d j -> p (c d j)"),
             )
+            block_codes[b] = nf1_codes
+            block_scales[b] = nf1_scales
 
+        dz_00 = mask_piece(0, 0)
+        dz_01 = mask_piece(0, 1)
+        quantise_piece(0, 0, dz_00)
+        dz_10 = mask_piece(1, 0)
+        quantise_piece(0, 1, dz_01)
+        dz_11 = mask_piece(1, 1)
+        quantise_piece(1, 0, dz_10)
+        block_grouped = {0: regroup_block(0)}
+        quantise_piece(1, 1, dz_11)
+        quantise_block(0, block_grouped[0])
+        block_grouped[1] = regroup_block(1)
+
+        for b in range(D_BLOCKS):
+            if b + 2 < D_BLOCKS:
+                block_grouped[b + 2] = regroup_block(b + 2)
+            if b + 1 < D_BLOCKS:
+                quantise_block(b + 1, block_grouped[b + 1])
+            rows = slice(b * D_BLOCK, (b + 1) * D_BLOCK)
+            in_halves = b in (0, D_BLOCKS - 1)
             result = results.tile([P, H], F32)
             for n in range(H_PIECES):
                 acc = psum.tile([P, H_PIECE], F32)
                 for c in range(PASSES):
                     nc.tensor.matmul_mx(
                         out=acc[:],
-                        lhsT=nf1_codes[:, c, :].bitcast(E4M3_X4),
-                        lhsT_scale=nf1_scales[:, c, :],
+                        lhsT=block_codes[b][:, c, :].bitcast(E4M3_X4),
+                        lhsT_scale=block_scales[b][:, c, :],
                         rhs=dz_codes[(c, n)][:].bitcast(E5M2_X4),
                         rhs_scale=dz_scales[(c, n)][:],
                         start=(c == 0),
                         stop=(c == PASSES - 1),
                     )
-                nc.scalar.copy(out=result[:, n * H_PIECE : (n + 1) * H_PIECE], in_=acc[:])
-            nc.sync.dma_start(out=out[b * D_BLOCK : (b + 1) * D_BLOCK, :], in_=result[:])
+                half = slice(n * H_PIECE, (n + 1) * H_PIECE)
+                nc.scalar.copy(out=result[:, half], in_=acc[:])
+                if in_halves:
+                    nc.sync.dma_start(out=out[rows, half], in_=result[:, half])
+            if not in_halves:
+                nc.sync.dma_start(out=out[rows, :], in_=result[:])

@@ -22,10 +22,11 @@ PASSES = NODES // K_PASS
 H_PIECE = 512
 H_PIECES = H // H_PIECE
 MASK_COLS = 256
-RUN = 4
+PAIR = 2
+PAIRS = PACK // PAIR
 D_BLOCK = P
 D_BLOCKS = D // D_BLOCK
-D_FIRST_CHUNK = 256
+D_CHUNKS = (256, 512, 1280)
 
 FLOPS = 2 * NODES * D * H
 BYTES = NODES * D * 2 + NODES * H * 4 + NODES * H * 2 + D * H * 4
@@ -58,15 +59,12 @@ def tile_graphsage_pa_v_kernel(tc, nf1, nf2, w1_0, w2_0, z, grad_out, out):
         load_columns(g_source, g_rows, BF16, 0, 0, H, "g")
         load_columns(z_source, z_rows, F32, 0, 0, H_PIECE, "z")
         load_columns(z_source, z_rows, F32, 0, H_PIECE, H_PIECE, "z")
-        load_columns(g_source, g_rows, BF16, 1, 0, H_PIECE, "g")
+        load_columns(g_source, g_rows, BF16, 1, 0, H, "g")
         load_columns(z_source, z_rows, F32, 1, 0, H_PIECE, "z")
-        load_columns(g_source, g_rows, BF16, 1, H_PIECE, H_PIECE, "g")
-        load_columns(z_source, z_rows, F32, 1, H_PIECE, MASK_COLS, "z")
-        load_columns(z_source, z_rows, F32, 1, H_PIECE + MASK_COLS, MASK_COLS, "z")
+        load_columns(z_source, z_rows, F32, 1, H_PIECE, H_PIECE, "z")
         nf1_source = {}
         first_col = 0
-        width = D_FIRST_CHUNK
-        while first_col < D:
+        for width in D_CHUNKS:
             nf1_tile = loads.tile([P, PASSES, PACK, width], BF16, name="nf1_raw_%d" % first_col)
             for c in range(PASSES):
                 nc.sync.dma_start(
@@ -75,27 +73,26 @@ def tile_graphsage_pa_v_kernel(tc, nf1, nf2, w1_0, w2_0, z, grad_out, out):
             for col in range(0, width, D_BLOCK):
                 nf1_source[(first_col + col) // D_BLOCK] = (nf1_tile, col)
             first_col += width
-            width = first_col
 
         def mask_piece(c, n):
-            dz_rows = grouped.tile([P, PACK, H_PIECE], BF16)
-            dz_grouped = grouped.tile([P, H_PIECE, PACK], BF16, align_bytes=64)
+            dz_pairs = grouped.tile([P, PAIRS, H_PIECE], F32)
+            dz_grouped = grouped.tile([P, H_PIECE, PAIRS], F32, align_bytes=64)
+            pair_values = dz_pairs[:].bitcast(BF16).rearrange("p a (h b) -> p a h b", b=PAIR)
             for first in range(0, H_PIECE, MASK_COLS):
                 cols = slice(first, first + MASK_COLS)
                 z_tile, z_col = z_source[(c, n * H_PIECE + first)]
                 g_tile, g_col = g_source[(c, n * H_PIECE + first)]
-                nc.vector.scalar_tensor_tensor(
-                    out=dz_rows[:, :, cols],
-                    in0=z_tile[:, :, z_col : z_col + MASK_COLS],
-                    scalar=0.0,
-                    in1=g_tile[:, :, g_col : g_col + MASK_COLS],
-                    op0=ALU.is_gt,
-                    op1=ALU.mult,
-                )
-                nc.scalar.copy(
-                    out=dz_grouped[:, cols, :].rearrange("p (x i) j -> p x j i", i=RUN),
-                    in_=dz_rows[:, :, cols].rearrange("p j (x i) -> p x j i", i=RUN),
-                )
+                for a in range(PAIRS):
+                    pair_rows = slice(a * PAIR, (a + 1) * PAIR)
+                    nc.vector.scalar_tensor_tensor(
+                        out=pair_values[:, a, cols, :],
+                        in0=z_tile[:, pair_rows, z_col : z_col + MASK_COLS].rearrange("p b h -> p h b"),
+                        scalar=0.0,
+                        in1=g_tile[:, pair_rows, g_col : g_col + MASK_COLS].rearrange("p b h -> p h b"),
+                        op0=ALU.is_gt,
+                        op1=ALU.mult,
+                    )
+                nc.scalar.copy(out=dz_grouped[:, cols, :], in_=dz_pairs[:, :, cols].rearrange("p a h -> p h a"))
             return dz_grouped
 
         dz_codes = {}
@@ -107,7 +104,7 @@ def tile_graphsage_pa_v_kernel(tc, nf1, nf2, w1_0, w2_0, z, grad_out, out):
             nc.vector.quantize_mx(
                 out=codes[:].bitcast(E5M2_X4),
                 scales=scales[:],
-                in_=dz_grouped[:].rearrange("p h j -> p (h j)"),
+                in_=dz_grouped[:].rearrange("p h a -> p (h a)").bitcast(BF16),
             )
             dz_codes[(c, n)] = codes
             dz_scales[(c, n)] = scales

@@ -47,21 +47,14 @@ def tile_graphsage_pa_v_kernel(tc, nf1, nf2, w1_0, w2_0, z, grad_out, out):
         results = ctx.enter_context(tc.tile_pool(name="results", bufs=4))
         psum = ctx.enter_context(tc.psum_pool(name="psum", bufs=8))
 
-        z_source = {}
-        g_source = {}
-
-        def load_columns(source, rows, dtype, c, first, width, label):
-            raw = loads.tile([P, PACK, width], dtype, name="%s_raw_%d_%d" % (label, c, first))
-            nc.sync.dma_start(out=raw[:], in_=rows[c, :, :, first : first + width])
-            for col in range(0, width, MASK_COLS):
-                source[(c, first + col)] = (raw, col)
-
-        load_columns(g_source, g_rows, BF16, 0, 0, H, "g")
-        load_columns(z_source, z_rows, F32, 0, 0, H_PIECE, "z")
-        load_columns(z_source, z_rows, F32, 0, H_PIECE, H_PIECE, "z")
-        load_columns(g_source, g_rows, BF16, 1, 0, H, "g")
-        load_columns(z_source, z_rows, F32, 1, 0, H_PIECE, "z")
-        load_columns(z_source, z_rows, F32, 1, H_PIECE, H_PIECE, "z")
+        g_raw = {}
+        z_raw = {}
+        for c in range(PASSES):
+            g_raw[c] = loads.tile([P, PACK, H], BF16, name="g_raw_%d" % c)
+            nc.sync.dma_start(out=g_raw[c][:], in_=g_rows[c])
+            for a in range(PAIRS):
+                z_raw[(c, a)] = loads.tile([P, PAIR, H], F32, name="z_raw_%d_%d" % (c, a))
+                nc.sync.dma_start(out=z_raw[(c, a)][:], in_=z_rows[c, :, a * PAIR : (a + 1) * PAIR, :])
         nf1_source = {}
         first_col = 0
         for width in D_CHUNKS:
@@ -74,37 +67,54 @@ def tile_graphsage_pa_v_kernel(tc, nf1, nf2, w1_0, w2_0, z, grad_out, out):
                 nf1_source[(first_col + col) // D_BLOCK] = (nf1_tile, col)
             first_col += width
 
-        def mask_piece(c, n):
-            dz_pairs = grouped.tile([P, PAIRS, H_PIECE], F32)
-            dz_grouped = grouped.tile([P, H_PIECE, PAIRS], F32, align_bytes=64)
-            pair_values = dz_pairs[:].bitcast(BF16).rearrange("p a (h b) -> p a h b", b=PAIR)
-            for first in range(0, H_PIECE, MASK_COLS):
-                cols = slice(first, first + MASK_COLS)
-                z_tile, z_col = z_source[(c, n * H_PIECE + first)]
-                g_tile, g_col = g_source[(c, n * H_PIECE + first)]
-                for a in range(PAIRS):
-                    pair_rows = slice(a * PAIR, (a + 1) * PAIR)
-                    nc.vector.scalar_tensor_tensor(
-                        out=pair_values[:, a, cols, :],
-                        in0=z_tile[:, pair_rows, z_col : z_col + MASK_COLS].rearrange("p b h -> p h b"),
-                        scalar=0.0,
-                        in1=g_tile[:, pair_rows, g_col : g_col + MASK_COLS].rearrange("p b h -> p h b"),
-                        op0=ALU.is_gt,
-                        op1=ALU.mult,
-                    )
-                nc.scalar.copy(out=dz_grouped[:, cols, :], in_=dz_pairs[:, :, cols].rearrange("p a h -> p h a"))
-            return dz_grouped
+        dz_pairs = {}
+        dz_grouped = {}
+
+        def mask_pair(c, a, width):
+            if a == 0:
+                dz_pairs[c] = new_pairs()
+            pair_values = dz_pairs[c][:].bitcast(BF16).rearrange("p a (h b) -> p a h b", b=PAIR)
+            pair_rows = slice(a * PAIR, (a + 1) * PAIR)
+            for first in range(0, H, width):
+                cols = slice(first, first + width)
+                nc.vector.scalar_tensor_tensor(
+                    out=pair_values[:, a, cols, :],
+                    in0=z_raw[(c, a)][:, :, cols].rearrange("p b h -> p h b"),
+                    scalar=0.0,
+                    in1=g_raw[c][:, pair_rows, cols].rearrange("p b h -> p h b"),
+                    op0=ALU.is_gt,
+                    op1=ALU.mult,
+                )
+                if a == PAIRS - 1:
+                    interleave_pairs(c, first, width)
+
+        def new_pairs():
+            pairs = grouped.tile([P, PAIRS, H], F32)
+            return pairs
+
+        def new_grouped():
+            words = grouped.tile([P, H_PIECE, PAIRS], F32, align_bytes=64)
+            return words
+
+        def interleave_pairs(c, first, width):
+            n, col = divmod(first, H_PIECE)
+            if col == 0:
+                dz_grouped[(c, n)] = new_grouped()
+            nc.scalar.copy(
+                out=dz_grouped[(c, n)][:, col : col + width, :],
+                in_=dz_pairs[c][:, :, first : first + width].rearrange("p a h -> p h a"),
+            )
 
         dz_codes = {}
         dz_scales = {}
 
-        def quantise_piece(c, n, dz_grouped):
+        def quantise_piece(c, n):
             codes = dz_mx.tile([P, H_PIECE], U32, tag="dz_codes", align_bytes=64)
             scales = dz_mx.tile([P, H_PIECE], U8, tag="dz_scales", align_bytes=64)
             nc.vector.quantize_mx(
                 out=codes[:].bitcast(E5M2_X4),
                 scales=scales[:],
-                in_=dz_grouped[:].rearrange("p h a -> p (h a)").bitcast(BF16),
+                in_=dz_grouped[(c, n)][:].rearrange("p h a -> p (h a)").bitcast(BF16),
             )
             dz_codes[(c, n)] = codes
             dz_scales[(c, n)] = scales
@@ -132,15 +142,15 @@ def tile_graphsage_pa_v_kernel(tc, nf1, nf2, w1_0, w2_0, z, grad_out, out):
             block_codes[b] = nf1_codes
             block_scales[b] = nf1_scales
 
-        dz_00 = mask_piece(0, 0)
-        dz_01 = mask_piece(0, 1)
-        quantise_piece(0, 0, dz_00)
-        dz_10 = mask_piece(1, 0)
-        quantise_piece(0, 1, dz_01)
-        dz_11 = mask_piece(1, 1)
-        quantise_piece(1, 0, dz_10)
+        mask_pair(0, 0, H_PIECE)
+        mask_pair(0, 1, MASK_COLS)
+        quantise_piece(0, 0)
+        quantise_piece(0, 1)
+        mask_pair(1, 0, H_PIECE)
+        mask_pair(1, 1, MASK_COLS)
+        quantise_piece(1, 0)
         block_grouped = {0: regroup_block(0)}
-        quantise_piece(1, 1, dz_11)
+        quantise_piece(1, 1)
         quantise_block(0, block_grouped[0])
         block_grouped[1] = regroup_block(1)
 

@@ -24,6 +24,7 @@ H_PIECES = H // H_PIECE
 MASK_COLS = 256
 PAIR = 2
 PAIRS = PACK // PAIR
+WARM_UPS = 2
 D_BLOCK = P
 D_BLOCKS = D // D_BLOCK
 D_CHUNKS = (256, 512, 1280)
@@ -87,6 +88,12 @@ def tile_graphsage_pa_v_kernel(tc, nf1, nf2, w1_0, w2_0, z, grad_out, out):
                 )
                 if a == PAIRS - 1:
                     interleave_pairs(c, first, width)
+                    if c == PASSES - 1:
+                        warm_up(dz_pairs[c][:, a, cols].bitcast(BF16))
+
+        def warm_up(values):
+            for i in range(WARM_UPS):
+                nc.tensor.matmul(out=warm_bank[:], lhsT=values[:, 0:P], rhs=values[:, 0:H_PIECE], start=True, stop=True)
 
         def new_pairs():
             pairs = grouped.tile([P, PAIRS, H], F32)
@@ -142,12 +149,14 @@ def tile_graphsage_pa_v_kernel(tc, nf1, nf2, w1_0, w2_0, z, grad_out, out):
             block_codes[b] = nf1_codes
             block_scales[b] = nf1_scales
 
+        warm_bank = psum.tile([P, H_PIECE], F32, tag="acc")
         mask_pair(0, 0, H_PIECE)
         mask_pair(0, 1, MASK_COLS)
         quantise_piece(0, 0)
         quantise_piece(0, 1)
         mask_pair(1, 0, H_PIECE)
         mask_pair(1, 1, MASK_COLS)
+        warm_up(dz_grouped[(1, 1)][:, H_PIECE - P :, :].rearrange("p h a -> p (h a)").bitcast(BF16))
         quantise_piece(1, 0)
         block_grouped = {0: regroup_block(0)}
         quantise_piece(1, 1)

from contextlib import ExitStack

import concourse.mybir as mybir

F32 = mybir.dt.float32
BF16 = mybir.dt.bfloat16
U32 = mybir.dt.uint32
U8 = mybir.dt.uint8
E4M3_X4 = mybir.dt.float8_e4m3fn_x4
E5M2_X4 = mybir.dt.float8_e5m2_x4
ALU = mybir.AluOpType

P = 128
PACK = 4
K_PASS = P * PACK

NODES = 1024
D = 2048
H = 1024
PASSES = NODES // K_PASS

H_PIECE = 512
H_PIECES = H // H_PIECE
MASK_COLS = 256
PAIR = 2
PAIRS = PACK // PAIR
WARM_UPS = 2
D_BLOCK = P
D_BLOCKS = D // D_BLOCK
D_CHUNKS = (256, 512, 1280)

FLOPS = 2 * NODES * D * H
BYTES = NODES * D * 2 + NODES * H * 4 + NODES * H * 2 + D * H * 4


def tile_graphsage_pa_v_kernel(tc, nf1, nf2, w1_0, w2_0, z, grad_out, out):
    nc = tc.nc

    z_rows = z.rearrange("(c p j) h -> c p j h", p=P, j=PACK)
    g_rows = grad_out.rearrange("(c p j) h -> c p j h", p=P, j=PACK)
    nf1_rows = nf1.rearrange("(c p j) d -> c p j d", p=P, j=PACK)

    with ExitStack() as ctx:
        loads = ctx.enter_context(tc.tile_pool(name="loads", bufs=1))
        grouped = ctx.enter_context(tc.tile_pool(name="grouped", bufs=3))
        dz_mx = ctx.enter_context(tc.tile_pool(name="dz_mx", bufs=PASSES * H_PIECES))
        nf1_mx = ctx.enter_context(tc.tile_pool(name="nf1_mx", bufs=4))
        results = ctx.enter_context(tc.tile_pool(name="results", bufs=4))
        psum = ctx.enter_context(tc.psum_pool(name="psum", bufs=8))

        g_raw = {}
        z_raw = {}
        for c in range(PASSES):
            g_raw[c] = loads.tile([P, PACK, H], BF16, name="g_raw_%d" % c)
            nc.sync.dma_start(out=g_raw[c][:], in_=g_rows[c])
            for a in range(PAIRS):
                z_raw[(c, a)] = loads.tile([P, PAIR, H], F32, name="z_raw_%d_%d" % (c, a))
                nc.sync.dma_start(out=z_raw[(c, a)][:], in_=z_rows[c, :, a * PAIR : (a + 1) * PAIR, :])
        nf1_source = {}
        first_col = 0
        for width in D_CHUNKS:
            nf1_tile = loads.tile([P, PASSES, PACK, width], BF16, name="nf1_raw_%d" % first_col)
            for c in range(PASSES):
                nc.sync.dma_start(
                    out=nf1_tile[:, c, :, :], in_=nf1_rows[c, :, :, first_col : first_col + width]
                )
            for col in range(0, width, D_BLOCK):
                nf1_source[(first_col + col) // D_BLOCK] = (nf1_tile, col)
            first_col += width

        dz_pairs = {}
        dz_grouped = {}

        def mask_pair(c, a, width):
            if a == 0:
                dz_pairs[c] = new_pairs()
            pair_values = dz_pairs[c][:].bitcast(BF16).rearrange("p a (h b) -> p a h b", b=PAIR)
            pair_rows = slice(a * PAIR, (a + 1) * PAIR)
            for first in range(0, H, width):
                cols = slice(first, first + width)
                nc.vector.scalar_tensor_tensor(
                    out=pair_values[:, a, cols, :],
                    in0=z_raw[(c, a)][:, :, cols].rearrange("p b h -> p h b"),
                    scalar=0.0,
                    in1=g_raw[c][:, pair_rows, cols].rearrange("p b h -> p h b"),
                    op0=ALU.is_gt,
                    op1=ALU.mult,
                )
                if a == PAIRS - 1:
                    interleave_pairs(c, first, width)
                    if c == PASSES - 1:
                        warm_up(dz_pairs[c][:, a, cols].bitcast(BF16))

        def warm_up(values):
            for i in range(WARM_UPS):
                nc.tensor.matmul(out=warm_bank[:], lhsT=values[:, 0:P], rhs=values[:, 0:H_PIECE], start=True, stop=True)

        def new_pairs():
            pairs = grouped.tile([P, PAIRS, H], F32)
            return pairs

        def new_grouped():
            words = grouped.tile([P, H_PIECE, PAIRS], F32, align_bytes=64)
            return words

        def interleave_pairs(c, first, width):
            n, col = divmod(first, H_PIECE)
            if col == 0:
                dz_grouped[(c, n)] = new_grouped()
            nc.scalar.copy(
                out=dz_grouped[(c, n)][:, col : col + width, :],
                in_=dz_pairs[c][:, :, first : first + width].rearrange("p a h -> p h a"),
            )

        dz_codes = {}
        dz_scales = {}

        def quantise_piece(c, n):
            codes = dz_mx.tile([P, H_PIECE], U32, tag="dz_codes", align_bytes=64)
            scales = dz_mx.tile([P, H_PIECE], U8, tag="dz_scales", align_bytes=64)
            nc.vector.quantize_mx(
                out=codes[:].bitcast(E5M2_X4),
                scales=scales[:],
                in_=dz_grouped[(c, n)][:].rearrange("p h a -> p (h a)").bitcast(BF16),
            )
            dz_codes[(c, n)] = codes
            dz_scales[(c, n)] = scales

        def regroup_block(b):
            nf1_tile, col = nf1_source[b]
            nf1_grouped = grouped.tile([P, PASSES, D_BLOCK, PACK], BF16, align_bytes=64)
            nc.vector.tensor_copy(
                out=nf1_grouped[:],
                in_=nf1_tile[:, :, :, col : col + D_BLOCK].rearrange("p c j d -> p c d j"),
            )
            return nf1_grouped

        block_codes = {}
        block_scales = {}

        def quantise_block(b, nf1_grouped):
            nf1_codes = nf1_mx.tile([P, PASSES, D_BLOCK], U32, align_bytes=64)
            nf1_scales = nf1_mx.tile([P, PASSES, D_BLOCK], U8, align_bytes=64)
            nc.vector.quantize_mx(
                out=nf1_codes[:].rearrange("p c d -> p (c d)").bitcast(E4M3_X4),
                scales=nf1_scales[:].rearrange("p c d -> p (c d)"),
                in_=nf1_grouped[:].rearrange("p c d j -> p (c d j)"),
            )
            block_codes[b] = nf1_codes
            block_scales[b] = nf1_scales

        warm_bank = psum.tile([P, H_PIECE], F32, tag="acc")
        mask_pair(0, 0, H_PIECE)
        mask_pair(0, 1, MASK_COLS)
        quantise_piece(0, 0)
        quantise_piece(0, 1)
        mask_pair(1, 0, H_PIECE)
        mask_pair(1, 1, MASK_COLS)
        warm_up(dz_grouped[(1, 1)][:, H_PIECE - P :, :].rearrange("p h a -> p (h a)").bitcast(BF16))
        quantise_piece(1, 0)
        block_grouped = {0: regroup_block(0)}
        quantise_piece(1, 1)
        quantise_block(0, block_grouped[0])
        block_grouped[1] = regroup_block(1)

        for b in range(D_BLOCKS):
            if b + 2 < D_BLOCKS:
                block_grouped[b + 2] = regroup_block(b + 2)
            if b + 1 < D_BLOCKS:
                quantise_block(b + 1, block_grouped[b + 1])
            rows = slice(b * D_BLOCK, (b + 1) * D_BLOCK)
            in_halves = b in (0, D_BLOCKS - 1)
            result = results.tile([P, H], F32)
            for n in range(H_PIECES):
                acc = psum.tile([P, H_PIECE], F32)
                for c in range(PASSES):
                    nc.tensor.matmul_mx(
                        out=acc[:],
                        lhsT=block_codes[b][:, c, :].bitcast(E4M3_X4),
                        lhsT_scale=block_scales[b][:, c, :],
                        rhs=dz_codes[(c, n)][:].bitcast(E5M2_X4),
                        rhs_scale=dz_scales[(c, n)][:],
                        start=(c == 0),
                        stop=(c == PASSES - 1),
                    )
                half = slice(n * H_PIECE, (n + 1) * H_PIECE)
                nc.scalar.copy(out=result[:, half], in_=acc[:])
                if in_halves:
                    nc.sync.dma_start(out=out[rows, half], in_=result[:, half])
            if not in_halves:
                nc.sync.dma_start(out=out[rows, :], in_=result[:])
